import numpy as np
import ml_dtypes


def mxq(x, axis, fmt="e4m3"):
    dtype, down = {"e4m3": (ml_dtypes.float8_e4m3fn, 7), "e5m2": (ml_dtypes.float8_e5m2, 14)}[fmt]
    v = np.moveaxis(np.asarray(x, np.float32).astype(ml_dtypes.bfloat16).astype(np.float64), axis, -1)
    blocks = v.reshape(v.shape[:-1] + (-1, 32))
    amax = np.abs(blocks).max(-1, keepdims=True)
    byte = np.maximum(np.where(amax > 0, np.frexp(amax)[1] - 1 + 127, 0) - down, 1)
    scale = np.exp2(byte - 127.0)
    codes = (blocks / scale).astype(np.float32).astype(dtype).astype(np.float64)
    return np.moveaxis((codes * scale).reshape(v.shape), -1, axis)


WIDE = False


def mx_kscale(k):
    if not WIDE:
        return np.ones(k)
    levels = np.array([10, -10, 5, -5, 0])
    a = np.random.permutation(np.resize(levels, k // 512 * 4)).reshape(k // 512, 4)
    idx = np.arange(k)
    return np.exp2(a[idx // 512, idx % 128 // 32])


BF16 = ml_dtypes.bfloat16


def bf(x):
    return np.asarray(x, np.float32).astype(BF16)


def f64(x):
    return np.asarray(x).astype(np.float64)


E2M1 = np.array([0.0, 0.5, 1.0, 1.5, 2.0, 3.0, 4.0, 6.0, -0.0, -0.5, -1.0, -1.5, -2.0, -3.0, -4.0, -6.0])


def pack_weight(w, fmt):
    k, n = w.shape
    w = f64(bf(w)).reshape(k // 32, 32, n)
    amax = np.abs(w).max(1)
    if fmt == "e4m3":
        byte = np.frexp(amax)[1] - 1 + 127 - 7
    else:
        mant, ex = np.frexp(amax / 6.0)
        byte = np.where(mant > 0.5, ex, ex - 1) + 127
    byte = np.clip(np.where(amax > 0, byte, 1), 1, 254)
    scaled = (w * np.exp2(127.0 - byte)[:, None, :]).reshape(k, n).astype(np.float32)
    by_word = np.ascontiguousarray(scaled.reshape(k // 512, 128, 4, n).transpose(0, 1, 3, 2))
    if fmt == "e4m3":
        words = by_word.astype(ml_dtypes.float8_e4m3fn).view(np.uint8)
    else:
        c = by_word.astype(ml_dtypes.float4_e2m1fn).view(np.uint8) & 0xF
        words = c[..., 0::2] | (c[..., 1::2] << 4)
    return np.ascontiguousarray(words), np.ascontiguousarray(byte.astype(np.uint8).reshape(k // 512, 16, n))


def unpack_weight(words, scales, fmt):
    g, p, n, _ = words.shape
    if fmt == "e4m3":
        vals = np.ascontiguousarray(words).view(ml_dtypes.float8_e4m3fn).astype(np.float64)
    else:
        nib = np.empty((g, p, n, 4), np.uint8)
        nib[..., 0::2] = words & 0xF
        nib[..., 1::2] = words >> 4
        vals = E2M1[nib]
    vals = vals * np.repeat(np.exp2(scales.astype(np.float64) - 127.0), 8, axis=1)[..., None]
    return vals.transpose(0, 1, 3, 2).reshape(g * 512, n)


B, L, H, U = 1, 256, 2048, 4096
R_MIN, R_MAX = 0.9, 0.999
FMT = "e4m3"


def setup_inputs():
    s, t = mx_kscale(H), mx_kscale(U)
    inputs = np.random.standard_normal((B, L, H)) * s
    Wi = np.random.standard_normal((U, H)) / np.sqrt(H) / s[None, :] * t[:, None]
    bi = np.random.standard_normal(U) * 0.03 * t
    Wo = np.random.standard_normal((H, U)) / np.sqrt(U) / t[None, :]
    bo = np.random.standard_normal(H) * 0.1
    r = np.random.uniform(size=U)
    nu_log = np.log(-0.5 * np.log(r * (R_MAX ** 2 - R_MIN ** 2) + R_MIN ** 2))
    gamma_log = np.log(np.sqrt(1.0 - np.exp(-np.exp(nu_log)) ** 2))
    params_log = np.stack([nu_log, gamma_log])
    Wi_words, Wi_scales = pack_weight(Wi.T, FMT)
    Wo_words, Wo_scales = pack_weight(Wo.T, FMT)
    return {"inputs": bf(inputs), "Wi_words": Wi_words, "Wi_scales": Wi_scales, "bi": bf(bi), "Wo_words": Wo_words, "Wo_scales": Wo_scales, "bo": bf(bo), "params_log": bf(params_log)}


def reference(inputs, Wi_words, Wi_scales, bi, Wo_words, Wo_scales, bo, params_log):
    u = (mxq(f64(inputs), 2, "e4m3") @ unpack_weight(Wi_words, Wi_scales, FMT)) + f64(bi)
    params = np.exp(f64(params_log))
    nu, gamma = params[0], params[1]

    log2_L = int(np.ceil(np.log2(L)))
    pad_len = 2 ** log2_L - L
    x = np.pad(u, ((0, 0), (0, pad_len), (0, 0))) if pad_len else u
    Lp = 2 ** log2_L

    for i in range(1, log2_L + 1):
        l = 2 ** i
        x = x.reshape(B * Lp // l, l, U)
        x1, x2 = x[:, : l // 2], x[:, l // 2:]
        pos = np.arange(1, l // 2 + 1, dtype=np.float64)
        lambs = np.exp(-pos[:, None] * nu)
        x2 = x2 + lambs * x1[:, -1:]
        x = np.concatenate([x1, x2], axis=1).reshape(B, Lp, U)

    x = x[:, :L] * gamma
    return (mxq(x, 2, "e4m3") @ unpack_weight(Wo_words, Wo_scales, FMT)) + f64(bo)

@@ -1,0 +1,357 @@
+from contextlib import ExitStack
+
+import concourse.mybir as mybir
+from concourse.masks import make_identity
+
+F32 = mybir.dt.float32
+BF16 = mybir.dt.bfloat16
+I32 = mybir.dt.int32
+U32 = mybir.dt.uint32
+U8 = mybir.dt.uint8
+FP8X4 = mybir.dt.float8_e4m3fn_x4
+ACT = mybir.ActivationFunctionType
+ALU = mybir.AluOpType
+
+P = 128
+L = 256
+H = 2048
+U = 4096
+KP = 512
+TT = L // P
+G1 = H // KP
+G2 = U // KP
+NT = H // 512
+
+FLOPS = 2 * L * H * U * 2
+
+PIECE_UNITS = (0, 1, 2)
+CHUNKS = ((3,), (4,), (5,), (6, 7))
+VECTOR_REGROUP = (0, 1, 2)
+K_SPLIT = 6
+
+
+def tile_slru_w_kernel(tc, inputs, Wi_words, Wi_scales, bi, Wo_words, Wo_scales, bo, params_log, out):
+    nc = tc.nc
+    with ExitStack() as ctx:
+        keep = ctx.enter_context(tc.tile_pool(name="keep", bufs=1))
+        two = ctx.enter_context(tc.tile_pool(name="two", bufs=2))
+        three = ctx.enter_context(tc.tile_pool(name="three", bufs=3))
+        five = ctx.enter_context(tc.tile_pool(name="five", bufs=5))
+        eight = ctx.enter_context(tc.tile_pool(name="eight", bufs=8))
+        psum = ctx.enter_context(tc.psum_pool(name="psum", bufs=1))
+        ctx.enter_context(tc.manual_schedule())
+
+        def bank(b, shape, dtype, name):
+            return psum.tile(shape, dtype, tag="bank%d" % b, name=name)
+
+        x_view = inputs.rearrange("b (tt p) k -> p (b tt) k", p=P)
+        w1_view = Wi_words.rearrange("g p n t -> p g (n t)").bitcast(I32)
+        w2_view = Wo_words.rearrange("g p n t -> p g (n t)").bitcast(I32)
+        s1_view = Wi_scales.bitcast(I32)
+        s2_view = Wo_scales.bitcast(I32)
+        par_view = params_log.rearrange("a (g c) -> (a g) c", c=KP)
+        bi_view = bi.rearrange("(g c) -> g c", c=KP)
+        bo_view = bo.rearrange("(o n) -> o n", o=1)
+        out_view = out.rearrange("b (tt p) n -> p (b tt) n", p=P)
+
+        ident_f = keep.tile([P, P], F32, name="ident_f")
+        ident_b = keep.tile([P, P], BF16, name="ident_b")
+        ones_b = keep.tile([P, P], BF16, name="ones_b")
+        make_identity(nc, ident_f[:])
+        make_identity(nc, ident_b[:])
+        nc.gpsimd.memset(ones_b[:], 1.0)
+
+        par_rows = keep.tile([P, KP], BF16, name="par_rows")
+        bo_rows = keep.tile([P, H], BF16, name="bo_rows")
+        junk = keep.tile([P, 1], F32, name="junk")
+        junk2 = keep.tile([P, 1], F32, name="junk2")
+        pl1 = [keep.tile([P, U // 2], U8, name="pl1_%d" % hf, align_bytes=64) for hf in range(2)]
+        pl2 = keep.tile([P, 2, H], U8, name="pl2", align_bytes=64)
+        nc.vector.memset(par_rows[:], 0.0)
+        nc.vector.memset(junk[:], 0.0)
+        nc.vector.memset(bo_rows[:], 0.0)
+        nc.vector.memset(pl1[0][:].bitcast(I32), 0)
+        nc.vector.memset(pl1[1][:].bitcast(I32), 0)
+        nc.vector.memset(pl2[:].rearrange("p a n -> p (a n)").bitcast(I32), 0)
+
+        nc.scalar.dma_start(out=par_rows[0:16, :], in_=par_view)
+        nc.scalar.dma_start(out=par_rows[16:24, :], in_=bi_view)
+        nc.scalar.dma_start(out=bo_rows[0:1, :], in_=bo_view)
+        nc.scalar.activation(out=junk2[:], in_=junk[:], func=ACT.Exp)
+
+        xin = [keep.tile([P, TT, H // 2], BF16, name="xin%d" % hf) for hf in range(2)]
+        for hf in range(2):
+            nc.sync.dma_start(out=xin[hf][:], in_=x_view[:, :, 1024 * hf : 1024 * hf + 1024])
+
+        def load_scales1(hf):
+            for q in range(4):
+                nc.sync.dma_start(
+                    out=pl1[hf][32 * q : 32 * q + 16, :].bitcast(I32),
+                    in_=s1_view[:, 4 * q : 4 * q + 4, 512 * hf : 512 * hf + 512],
+                )
+
+        w1 = {}
+        load_scales1(0)
+        for j in PIECE_UNITS:
+            for g in range(G1):
+                piece = keep.tile([P, 512], U32, name="w1_%d_%d" % (j, g), align_bytes=64)
+                nc.sync.dma_start(out=piece[:].bitcast(I32), in_=w1_view[:, g, 512 * j : 512 * j + 512])
+                w1[(j, g)] = piece[:]
+        for units in CHUNKS:
+            if units[0] == 4:
+                load_scales1(1)
+            width = 512 * len(units)
+            chunk = keep.tile([P, G1, width], U32, name="w1_c%d" % units[0], align_bytes=64)
+            nc.sync.dma_start(
+                out=chunk[:].bitcast(I32), in_=w1_view[:, :, 512 * units[0] : 512 * units[0] + width]
+            )
+            for i, j in enumerate(units):
+                for g in range(G1):
+                    w1[(j, g)] = chunk[:, g, 512 * i : 512 * i + 512]
+        for a in range(2):
+            for q in range(4):
+                nc.sync.dma_start(
+                    out=pl2[32 * q : 32 * q + 16, a, :].bitcast(I32),
+                    in_=s2_view[4 * a : 4 * a + 4, 4 * q : 4 * q + 4, :],
+                )
+        w2 = []
+        for g in range(G2):
+            words = keep.tile([P, H], U32, name="w2_%d" % g, align_bytes=64)
+            nc.sync.dma_start(out=words[:].bitcast(I32), in_=w2_view[:, g, :])
+            w2.append(words)
+
+        xt = [bank(2 + g, [P, 2, L], F32, "xt%d" % g) for g in range(G1)]
+        gi = [five.tile([P, 4 * L], BF16, tag="b2k", name="gi%d" % g, align_bytes=64) for g in range(G1)]
+        xq1 = [keep.tile([P, L], U32, name="xq1_%d" % g, align_bytes=64) for g in range(G1)]
+        xs1 = [keep.tile([P, L], U8, name="xs1_%d" % g, align_bytes=64) for g in range(G1)]
+
+        def in_transposes(g):
+            words = xin[g // 2][:].rearrange("p tt k -> p (tt k)").bitcast(F32)
+            for u in range(2):
+                for tt in range(TT):
+                    base = 512 * tt + 256 * (g % 2)
+                    nc.tensor.transpose(
+                        out=xt[g][:, u, P * tt : P * tt + P],
+                        in_=words[:, base + u : base + 256 : 2],
+                        identity=ident_f[:],
+                    )
+
+        def in_regroup(g, on_vector):
+            dst = gi[g][:].bitcast(F32).rearrange("p (w u) -> p w u", u=2)
+            src = xt[g][:].rearrange("p u w -> p w u")
+            if on_vector:
+                nc.vector.tensor_copy(out=dst, in_=src)
+            else:
+                nc.scalar.copy(out=dst, in_=src)
+
+        def in_quantise(g):
+            nc.vector.quantize_mx(out=xq1[g][:].bitcast(FP8X4), scales=xs1[g][:], in_=gi[g][:])
+
+        pp = bank(7, [P, 4, P], BF16, "pp")
+        eg = keep.tile([P, 4, 16], F32, name="eg")
+        th = keep.tile([P, 4, 8], F32, name="th")
+        den = keep.tile([P, 4, 8], F32, name="den")
+        num = keep.tile([P, 4, 8], F32, name="num")
+        rden = keep.tile([P, 4, 8], F32, name="rden")
+        lam = keep.tile([P, 4, 8], F32, name="lam")
+        gb = keep.tile([P, 4, 8], F32, name="gb")
+
+        in_transposes(0)
+        in_transposes(1)
+        for t in range(4):
+            nc.tensor.transpose(out=pp[:, t, :], in_=par_rows[:, t:KP:4], identity=ident_b[:])
+        in_regroup(0, True)
+        in_regroup(1, False)
+        nc.scalar.activation(out=eg[:], in_=pp[:, :, 0:16], func=ACT.Exp)
+        nc.scalar.activation(out=th[:], in_=eg[:, :, 0:8], func=ACT.Tanh, scale=0.5)
+        in_transposes(2)
+        in_transposes(3)
+        in_quantise(0)
+        nc.vector.tensor_tensor(out=gb[:], in0=eg[:, :, 8:16], in1=pp[:, :, 16:24], op=ALU.mult)
+        in_regroup(2, True)
+        in_regroup(3, False)
+        in_quantise(1)
+        in_quantise(2)
+        nc.vector.tensor_scalar_add(out=den[:], in0=th[:], scalar1=1.0)
+        nc.vector.tensor_scalar(out=num[:], in0=th[:], scalar1=-1.0, scalar2=1.0, op0=ALU.mult, op1=ALU.add)
+        in_quantise(3)
+        nc.vector.reciprocal(out=rden[:], in_=den[:])
+        nc.vector.tensor_tensor(out=lam[:], in0=num[:], in1=rden[:], op=ALU.mult)
+
+        acc = {}
+        u_sb = {}
+        vt = {}
+        v_sb = {}
+        xb = {}
+        xg = {}
+        xq2 = [keep.tile([P, L], U32, name="xq2_%d" % j, align_bytes=64) for j in range(G2)]
+        xs2 = [keep.tile([P, L], U8, name="xs2_%d" % j, align_bytes=64) for j in range(G2)]
+        bo_bc = [keep.tile([P, 1024], F32, name="bo_bc%d" % i) for i in range(2)]
+
+        def pass1(j, tt, g):
+            if g == 0:
+                acc[(j, tt)] = bank(2 * (j % 2) + tt, [P, 512], F32, "acc_%d_%d" % (j, tt))
+            nc.tensor.matmul_mx(
+                out=acc[(j, tt)][:],
+                lhsT=xq1[g][:, P * tt : P * tt + P].bitcast(FP8X4),
+                lhsT_scale=xs1[g][:, P * tt : P * tt + P],
+                rhs=w1[(j, g)].bitcast(FP8X4),
+                rhs_scale=pl1[j // 4][4 * g : P, 512 * (j % 4) : 512 * (j % 4) + 512],
+                start=(g == 0),
+                stop=(g == G1 - 1),
+            )
+
+        def sort_out(j, tt):
+            u_sb[(j, tt)] = two.tile([P, 4, P], F32, tag="u%d" % tt, name="u_%d_%d" % (j, tt))
+            nc.scalar.copy(out=u_sb[(j, tt)][:], in_=acc[(j, tt)][:].rearrange("p (c t) -> p t c", t=4))
+
+        def transposes(j):
+            for hb in range(2):
+                vt[(j, hb)] = bank(4 + 2 * (j % 2) + hb, [P, 2, L], F32, "vt_%d_%d" % (j, hb))
+            for t in range(4):
+                for tt in range(TT):
+                    nc.tensor.transpose(
+                        out=vt[(j, t // 2)][:, t % 2, P * tt : P * tt + P],
+                        in_=u_sb[(j, tt)][:, t, :],
+                        identity=ident_f[:],
+                    )
+
+        def scale_bias(j, t):
+            v_sb[(j, t)] = three.tile([P, L], F32, tag="v%d" % t, name="v_%d_%d" % (j, t))
+            nc.scalar.activation(
+                out=v_sb[(j, t)][:],
+                in_=vt[(j, t // 2)][:, t % 2, :],
+                func=ACT.Identity,
+                bias=gb[:, t, j : j + 1],
+                scale=eg[:, t, 8 + j : 9 + j],
+            )
+
+        def scan(j, t):
+            if t == 0:
+                xb[j] = five.tile([P, 4, L], BF16, tag="b2k", name="xb%d" % j, align_bytes=64)
+            nc.vector.tensor_tensor_scan(
+                out=xb[j][:, t, :],
+                data0=lam[:, t, j : j + 1].to_broadcast([P, L]),
+                data1=v_sb[(j, t)][:],
+                initial=0.0,
+                op0=ALU.mult,
+                op1=ALU.add,
+            )
+
+        def regroup(j):
+            xg[j] = two.tile([P, L, 4], BF16, tag="xg", name="xg%d" % j, align_bytes=64)
+            dst = xg[j][:].rearrange("p (c i) t -> p c t i", i=4)
+            src = xb[j][:].rearrange("p t (c i) -> p c t i", i=4)
+            if j in VECTOR_REGROUP:
+                nc.vector.tensor_copy(out=dst, in_=src)
+            else:
+                nc.scalar.copy(out=dst, in_=src)
+
+        def quantise(j):
+            nc.vector.quantize_mx(
+                out=xq2[j][:].bitcast(FP8X4), scales=xs2[j][:], in_=xg[j][:].rearrange("p w t -> p (w t)")
+            )
+
+        def spread_bo():
+            for i in range(2):
+                pb = bank(6 + i, [P, 1024], BF16, "pb%d" % i)
+                for k in range(2):
+                    nc.tensor.matmul(
+                        out=pb[:, 512 * k : 512 * k + 512],
+                        lhsT=ones_b[:],
+                        rhs=bo_rows[:, 1024 * i + 512 * k : 1024 * i + 512 * k + 512],
+                        start=True,
+                        stop=True,
+                    )
+                nc.vector.tensor_copy(out=bo_bc[i][:], in_=pb[:])
+
+        for j in range(G2):
+            if j in PIECE_UNITS:
+                order = [(tt, g) for g in range(G1) for tt in range(TT)]
+                cut = 6
+            else:
+                order = [(tt, g) for tt in range(TT) for g in range(G1)]
+                cut = 4
+            for tt, g in order[:cut]:
+                pass1(j, tt, g)
+            if j not in PIECE_UNITS:
+                sort_out(j, 0)
+            if j >= 1:
+                transposes(j - 1)
+                for t in range(4):
+                    scale_bias(j - 1, t)
+                for t in range(4):
+                    scan(j - 1, t)
+            for tt, g in order[cut:]:
+                pass1(j, tt, g)
+            if j in PIECE_UNITS:
+                sort_out(j, 0)
+            sort_out(j, 1)
+            if j == 0:
+                spread_bo()
+            if j - 3 in VECTOR_REGROUP:
+                quantise(j - 3)
+            if j - 2 in VECTOR_REGROUP:
+                regroup(j - 2)
+            if j == G2 - 1:
+                regroup(3)
+
+        o_ps = {}
+
+        def pass2(tt, n, g):
+            if g == 0:
+                o_ps[(tt, n)] = bank(2 * n + tt, [P, 512], F32, "o_%d_%d" % (tt, n))
+            nc.tensor.matmul_mx(
+                out=o_ps[(tt, n)][:],
+                lhsT=xq2[g][:, P * tt : P * tt + P].bitcast(FP8X4),
+                lhsT_scale=xs2[g][:, P * tt : P * tt + P],
+                rhs=w2[g][:, 512 * n : 512 * n + 512].bitcast(FP8X4),
+                rhs_scale=pl2[4 * (g % 4) : P, g // 4, 512 * n : 512 * n + 512],
+                start=(g == 0),
+                stop=(g == G2 - 1),
+            )
+
+        def round2(tiles, g):
+            for n in tiles:
+                for tt in range(TT):
+                    pass2(tt, n, g)
+
+        def finish(tt, n):
+            o_sb = eight.tile([P, 512], F32, tag="o", name="o_sb_%d_%d" % (tt, n))
+            nc.vector.tensor_tensor(
+                out=o_sb[:], in0=o_ps[(tt, n)][:], in1=bo_bc[n // 2][:, 512 * (n % 2) : 512 * (n % 2) + 512], op=ALU.add
+            )
+            nc.sync.dma_start(out=out_view[:, tt, 512 * n : 512 * n + 512], in_=o_sb[:])
+
+        last = G2 - 1
+        round2((0,), 0)
+        round2((0,), 1)
+        transposes(last)
+        for t in range(4):
+            scale_bias(last, t)
+        scan(last, 0)
+        quantise(3)
+        regroup(4)
+        scan(last, 1)
+        scan(last, 2)
+        quantise(4)
+        regroup(5)
+        scan(last, 3)
+        quantise(5)
+        regroup(6)
+        quantise(6)
+        regroup(7)
+        quantise(7)
+        round2((1,), 0)
+        round2((1,), 1)
+        round2((0, 1), 2)
+        for g in range(3):
+            round2((2, 3), g)
+        for g in range(3, K_SPLIT):
+            round2((0, 1), g)
+            round2((2, 3), g)
+        for n in range(NT):
+            for tt in range(TT):
+                for g in range(K_SPLIT, G2):
+                    pass2(tt, n, g)
+                finish(tt, n)

@@ -24,10 +24,11 @@ NT = H // 512
 
 FLOPS = 2 * L * H * U * 2
 
-PIECE_UNITS = (0, 1, 2)
-CHUNKS = ((3,), (4,), (5,), (6, 7))
+PIECE_UNITS = (0, 1, 2, 3, 4)
+CHUNK_UNITS = (5, 6, 7)
 VECTOR_REGROUP = (0, 1, 2)
-K_SPLIT = 6
+K_ROUND = (6, 6, 5, 5)
+O_BANK = (0, 4, 2, 6)
 
 
 def tile_slru_w_kernel(tc, inputs, Wi_words, Wi_scales, bi, Wo_words, Wo_scales, bo, params_log, out):
@@ -67,16 +68,16 @@ def tile_slru_w_kernel(tc, inputs, Wi_words, Wi_scales, bi, Wo_words, Wo_scales,
         junk2 = keep.tile([P, 1], F32, name="junk2")
         pl1 = [keep.tile([P, U // 2], U8, name="pl1_%d" % hf, align_bytes=64) for hf in range(2)]
         pl2 = keep.tile([P, 2, H], U8, name="pl2", align_bytes=64)
+        nc.vector.memset(bo_rows[:], 0.0)
         nc.vector.memset(par_rows[:], 0.0)
         nc.vector.memset(junk[:], 0.0)
-        nc.vector.memset(bo_rows[:], 0.0)
         nc.vector.memset(pl1[0][:].bitcast(I32), 0)
         nc.vector.memset(pl1[1][:].bitcast(I32), 0)
         nc.vector.memset(pl2[:].rearrange("p a n -> p (a n)").bitcast(I32), 0)
 
+        nc.scalar.dma_start(out=bo_rows[0:1, :], in_=bo_view)
         nc.scalar.dma_start(out=par_rows[0:16, :], in_=par_view)
         nc.scalar.dma_start(out=par_rows[16:24, :], in_=bi_view)
-        nc.scalar.dma_start(out=bo_rows[0:1, :], in_=bo_view)
         nc.scalar.activation(out=junk2[:], in_=junk[:], func=ACT.Exp)
 
         xin = [keep.tile([P, TT, H // 2], BF16, name="xin%d" % hf) for hf in range(2)]
@@ -93,32 +94,35 @@ def tile_slru_w_kernel(tc, inputs, Wi_words, Wi_scales, bi, Wo_words, Wo_scales,
         w1 = {}
         load_scales1(0)
         for j in PIECE_UNITS:
+            if j == 4:
+                load_scales1(1)
             for g in range(G1):
                 piece = keep.tile([P, 512], U32, name="w1_%d_%d" % (j, g), align_bytes=64)
                 nc.sync.dma_start(out=piece[:].bitcast(I32), in_=w1_view[:, g, 512 * j : 512 * j + 512])
                 w1[(j, g)] = piece[:]
-        for units in CHUNKS:
-            if units[0] == 4:
-                load_scales1(1)
-            width = 512 * len(units)
-            chunk = keep.tile([P, G1, width], U32, name="w1_c%d" % units[0], align_bytes=64)
-            nc.sync.dma_start(
-                out=chunk[:].bitcast(I32), in_=w1_view[:, :, 512 * units[0] : 512 * units[0] + width]
-            )
-            for i, j in enumerate(units):
-                for g in range(G1):
-                    w1[(j, g)] = chunk[:, g, 512 * i : 512 * i + 512]
+        for j in CHUNK_UNITS:
+            chunk = keep.tile([P, G1, 512], U32, name="w1_c%d" % j, align_bytes=64)
+            nc.sync.dma_start(out=chunk[:].bitcast(I32), in_=w1_view[:, :, 512 * j : 512 * j + 512])
+            for g in range(G1):
+                w1[(j, g)] = chunk[:, g, :]
         for a in range(2):
             for q in range(4):
                 nc.sync.dma_start(
                     out=pl2[32 * q : 32 * q + 16, a, :].bitcast(I32),
                     in_=s2_view[4 * a : 4 * a + 4, 4 * q : 4 * q + 4, :],
                 )
-        w2 = []
-        for g in range(G2):
-            words = keep.tile([P, H], U32, name="w2_%d" % g, align_bytes=64)
-            nc.sync.dma_start(out=words[:].bitcast(I32), in_=w2_view[:, g, :])
-            w2.append(words)
+        w2 = {}
+        for g in range(max(K_ROUND)):
+            tiles = [n for n in range(NT) if K_ROUND[n] > g]
+            words = keep.tile([P, 512 * len(tiles)], U32, name="w2_%d" % g, align_bytes=64)
+            nc.sync.dma_start(out=words[:].bitcast(I32), in_=w2_view[:, g, 0 : 512 * len(tiles)])
+            for n in tiles:
+                w2[(g, n)] = words[:, 512 * n : 512 * n + 512]
+        for n in range(NT):
+            words = keep.tile([P, G2 - K_ROUND[n], 512], U32, name="w2_end%d" % n, align_bytes=64)
+            nc.sync.dma_start(out=words[:].bitcast(I32), in_=w2_view[:, K_ROUND[n] : G2, 512 * n : 512 * n + 512])
+            for g in range(K_ROUND[n], G2):
+                w2[(g, n)] = words[:, g - K_ROUND[n], :]
 
         xt = [bank(2 + g, [P, 2, L], F32, "xt%d" % g) for g in range(G1)]
         gi = [five.tile([P, 4 * L], BF16, tag="b2k", name="gi%d" % g, align_bytes=64) for g in range(G1)]
@@ -147,7 +151,7 @@ def tile_slru_w_kernel(tc, inputs, Wi_words, Wi_scales, bi, Wo_words, Wo_scales,
         def in_quantise(g):
             nc.vector.quantize_mx(out=xq1[g][:].bitcast(FP8X4), scales=xs1[g][:], in_=gi[g][:])
 
-        pp = bank(7, [P, 4, P], BF16, "pp")
+        pp = bank(1, [P, 4, P], BF16, "pp")
         eg = keep.tile([P, 4, 16], F32, name="eg")
         th = keep.tile([P, 4, 8], F32, name="th")
         den = keep.tile([P, 4, 8], F32, name="den")
@@ -156,6 +160,17 @@ def tile_slru_w_kernel(tc, inputs, Wi_words, Wi_scales, bi, Wo_words, Wo_scales,
         lam = keep.tile([P, 4, 8], F32, name="lam")
         gb = keep.tile([P, 4, 8], F32, name="gb")
 
+        bo_bc = [keep.tile([P, 1024], F32, name="bo_bc%d" % i) for i in range(2)]
+        pb = [bank(6 + i, [P, 1024], BF16, "pb%d" % i) for i in range(2)]
+        for i in range(2):
+            for k in range(2):
+                nc.tensor.matmul(
+                    out=pb[i][:, 512 * k : 512 * k + 512],
+                    lhsT=ones_b[:],
+                    rhs=bo_rows[:, 1024 * i + 512 * k : 1024 * i + 512 * k + 512],
+                    start=True,
+                    stop=True,
+                )
         in_transposes(0)
         in_transposes(1)
         for t in range(4):
@@ -177,6 +192,8 @@ def tile_slru_w_kernel(tc, inputs, Wi_words, Wi_scales, bi, Wo_words, Wo_scales,
         in_quantise(3)
         nc.vector.reciprocal(out=rden[:], in_=den[:])
         nc.vector.tensor_tensor(out=lam[:], in0=num[:], in1=rden[:], op=ALU.mult)
+        for i in range(2):
+            nc.vector.tensor_copy(out=bo_bc[i][:], in_=pb[i][:])
 
         acc = {}
         u_sb = {}
@@ -186,7 +203,6 @@ def tile_slru_w_kernel(tc, inputs, Wi_words, Wi_scales, bi, Wo_words, Wo_scales,
         xg = {}
         xq2 = [keep.tile([P, L], U32, name="xq2_%d" % j, align_bytes=64) for j in range(G2)]
         xs2 = [keep.tile([P, L], U8, name="xs2_%d" % j, align_bytes=64) for j in range(G2)]
-        bo_bc = [keep.tile([P, 1024], F32, name="bo_bc%d" % i) for i in range(2)]
 
         def pass1(j, tt, g):
             if g == 0:
@@ -252,19 +268,6 @@ def tile_slru_w_kernel(tc, inputs, Wi_words, Wi_scales, bi, Wo_words, Wo_scales,
                 out=xq2[j][:].bitcast(FP8X4), scales=xs2[j][:], in_=xg[j][:].rearrange("p w t -> p (w t)")
             )
 
-        def spread_bo():
-            for i in range(2):
-                pb = bank(6 + i, [P, 1024], BF16, "pb%d" % i)
-                for k in range(2):
-                    nc.tensor.matmul(
-                        out=pb[:, 512 * k : 512 * k + 512],
-                        lhsT=ones_b[:],
-                        rhs=bo_rows[:, 1024 * i + 512 * k : 1024 * i + 512 * k + 512],
-                        start=True,
-                        stop=True,
-                    )
-                nc.vector.tensor_copy(out=bo_bc[i][:], in_=pb[:])
-
         for j in range(G2):
             if j in PIECE_UNITS:
                 order = [(tt, g) for g in range(G1) for tt in range(TT)]
@@ -287,8 +290,6 @@ def tile_slru_w_kernel(tc, inputs, Wi_words, Wi_scales, bi, Wo_words, Wo_scales,
             if j in PIECE_UNITS:
                 sort_out(j, 0)
             sort_out(j, 1)
-            if j == 0:
-                spread_bo()
             if j - 3 in VECTOR_REGROUP:
                 quantise(j - 3)
             if j - 2 in VECTOR_REGROUP:
@@ -300,12 +301,12 @@ def tile_slru_w_kernel(tc, inputs, Wi_words, Wi_scales, bi, Wo_words, Wo_scales,
 
         def pass2(tt, n, g):
             if g == 0:
-                o_ps[(tt, n)] = bank(2 * n + tt, [P, 512], F32, "o_%d_%d" % (tt, n))
+                o_ps[(tt, n)] = bank(O_BANK[n] + tt, [P, 512], F32, "o_%d_%d" % (tt, n))
             nc.tensor.matmul_mx(
                 out=o_ps[(tt, n)][:],
                 lhsT=xq2[g][:, P * tt : P * tt + P].bitcast(FP8X4),
                 lhsT_scale=xs2[g][:, P * tt : P * tt + P],
-                rhs=w2[g][:, 512 * n : 512 * n + 512].bitcast(FP8X4),
+                rhs=w2[(g, n)].bitcast(FP8X4),
                 rhs_scale=pl2[4 * (g % 4) : P, g // 4, 512 * n : 512 * n + 512],
                 start=(g == 0),
                 stop=(g == G2 - 1),
@@ -324,8 +325,7 @@ def tile_slru_w_kernel(tc, inputs, Wi_words, Wi_scales, bi, Wo_words, Wo_scales,
             nc.sync.dma_start(out=out_view[:, tt, 512 * n : 512 * n + 512], in_=o_sb[:])
 
         last = G2 - 1
-        round2((0,), 0)
-        round2((0,), 1)
+        round2((0, 1), 0)
         transposes(last)
         for t in range(4):
             scale_bias(last, t)
@@ -342,16 +342,15 @@ def tile_slru_w_kernel(tc, inputs, Wi_words, Wi_scales, bi, Wo_words, Wo_scales,
         quantise(6)
         regroup(7)
         quantise(7)
-        round2((1,), 0)
-        round2((1,), 1)
-        round2((0, 1), 2)
+        round2((2,), 0)
+        round2((0, 1, 2), 1)
+        round2((0, 1, 2), 2)
         for g in range(3):
-            round2((2, 3), g)
-        for g in range(3, K_SPLIT):
-            round2((0, 1), g)
-            round2((2, 3), g)
+            round2((3,), g)
+        for g in range(3, max(K_ROUND)):
+            round2([n for n in range(NT) if K_ROUND[n] > g], g)
         for n in range(NT):
             for tt in range(TT):
-                for g in range(K_SPLIT, G2):
+                for g in range(K_ROUND[n], G2):
                     pass2(tt, n, g)
                 finish(tt, n)

@@ -29,6 +29,7 @@ CHUNK_UNITS = (5, 6, 7)
 VECTOR_REGROUP = (0, 1, 2)
 K_ROUND = (6, 6, 5, 5)
 O_BANK = (0, 4, 2, 6)
+WARM_UP = 8
 
 
 def tile_slru_w_kernel(tc, inputs, Wi_words, Wi_scales, bi, Wo_words, Wo_scales, bo, params_log, out):
@@ -68,6 +69,8 @@ def tile_slru_w_kernel(tc, inputs, Wi_words, Wi_scales, bi, Wo_words, Wo_scales,
         junk2 = keep.tile([P, 1], F32, name="junk2")
         pl1 = [keep.tile([P, U // 2], U8, name="pl1_%d" % hf, align_bytes=64) for hf in range(2)]
         pl2 = keep.tile([P, 2, H], U8, name="pl2", align_bytes=64)
+        warm = keep.tile([P, 512], BF16, name="warm")
+        nc.vector.memset(warm[:], 0.0)
         nc.vector.memset(bo_rows[:], 0.0)
         nc.vector.memset(par_rows[:], 0.0)
         nc.vector.memset(junk[:], 0.0)
@@ -151,7 +154,7 @@ def tile_slru_w_kernel(tc, inputs, Wi_words, Wi_scales, bi, Wo_words, Wo_scales,
         def in_quantise(g):
             nc.vector.quantize_mx(out=xq1[g][:].bitcast(FP8X4), scales=xs1[g][:], in_=gi[g][:])
 
-        pp = bank(1, [P, 4, P], BF16, "pp")
+
         eg = keep.tile([P, 4, 16], F32, name="eg")
         th = keep.tile([P, 4, 8], F32, name="th")
         den = keep.tile([P, 4, 8], F32, name="den")
@@ -160,6 +163,11 @@ def tile_slru_w_kernel(tc, inputs, Wi_words, Wi_scales, bi, Wo_words, Wo_scales,
         lam = keep.tile([P, 4, 8], F32, name="lam")
         gb = keep.tile([P, 4, 8], F32, name="gb")
 
+        warm_ps = bank(0, [P, 512], F32, "warm_ps")
+        for i in range(WARM_UP):
+            nc.tensor.matmul(out=warm_ps[:], lhsT=warm[:, 0:P], rhs=warm[:], start=True, stop=True)
+        in_transposes(0)
+        in_transposes(1)
         bo_bc = [keep.tile([P, 1024], F32, name="bo_bc%d" % i) for i in range(2)]
         pb = [bank(6 + i, [P, 1024], BF16, "pb%d" % i) for i in range(2)]
         for i in range(2):
@@ -171,25 +179,24 @@ def tile_slru_w_kernel(tc, inputs, Wi_words, Wi_scales, bi, Wo_words, Wo_scales,
                     start=True,
                     stop=True,
                 )
-        in_transposes(0)
-        in_transposes(1)
-        for t in range(4):
-            nc.tensor.transpose(out=pp[:, t, :], in_=par_rows[:, t:KP:4], identity=ident_b[:])
         in_regroup(0, True)
         in_regroup(1, False)
-        nc.scalar.activation(out=eg[:], in_=pp[:, :, 0:16], func=ACT.Exp)
-        nc.scalar.activation(out=th[:], in_=eg[:, :, 0:8], func=ACT.Tanh, scale=0.5)
         in_transposes(2)
         in_transposes(3)
         in_quantise(0)
-        nc.vector.tensor_tensor(out=gb[:], in0=eg[:, :, 8:16], in1=pp[:, :, 16:24], op=ALU.mult)
         in_regroup(2, True)
         in_regroup(3, False)
         in_quantise(1)
         in_quantise(2)
+        in_quantise(3)
+        pp = bank(2, [P, 4, P], BF16, "pp")
+        for t in range(4):
+            nc.tensor.transpose(out=pp[:, t, :], in_=par_rows[:, t:KP:4], identity=ident_b[:])
+        nc.scalar.activation(out=eg[:], in_=pp[:, :, 0:16], func=ACT.Exp)
+        nc.scalar.activation(out=th[:], in_=eg[:, :, 0:8], func=ACT.Tanh, scale=0.5)
+        nc.vector.tensor_tensor(out=gb[:], in0=eg[:, :, 8:16], in1=pp[:, :, 16:24], op=ALU.mult)
         nc.vector.tensor_scalar_add(out=den[:], in0=th[:], scalar1=1.0)
         nc.vector.tensor_scalar(out=num[:], in0=th[:], scalar1=-1.0, scalar2=1.0, op0=ALU.mult, op1=ALU.add)
-        in_quantise(3)
         nc.vector.reciprocal(out=rden[:], in_=den[:])
         nc.vector.tensor_tensor(out=lam[:], in0=num[:], in1=rden[:], op=ALU.mult)
         for i in range(2):

@@ -24,11 +24,10 @@ NT = H // 512
 
 FLOPS = 2 * L * H * U * 2
 
-PIECE_UNITS = (0, 1, 2, 3, 4)
-CHUNK_UNITS = (5, 6, 7)
-VECTOR_REGROUP = (0, 1, 2)
+PIECE_UNITS = (0, 1, 2, 3)
+W_UNITS = (4, 5, 6, 7)
 K_ROUND = (6, 6, 5, 5)
-O_BANK = (0, 4, 2, 6)
+O_BANK = (0, 2, 4, 6)
 WARM_UP = 8
 
 
@@ -37,9 +36,8 @@ def tile_slru_w_kernel(tc, inputs, Wi_words, Wi_scales, bi, Wo_words, Wo_scales,
     with ExitStack() as ctx:
         keep = ctx.enter_context(tc.tile_pool(name="keep", bufs=1))
         two = ctx.enter_context(tc.tile_pool(name="two", bufs=2))
-        three = ctx.enter_context(tc.tile_pool(name="three", bufs=3))
+        four = ctx.enter_context(tc.tile_pool(name="four", bufs=4))
         five = ctx.enter_context(tc.tile_pool(name="five", bufs=5))
-        eight = ctx.enter_context(tc.tile_pool(name="eight", bufs=8))
         psum = ctx.enter_context(tc.psum_pool(name="psum", bufs=1))
         ctx.enter_context(tc.manual_schedule())
 
@@ -83,7 +81,7 @@ def tile_slru_w_kernel(tc, inputs, Wi_words, Wi_scales, bi, Wo_words, Wo_scales,
         nc.scalar.dma_start(out=par_rows[16:24, :], in_=bi_view)
         nc.scalar.activation(out=junk2[:], in_=junk[:], func=ACT.Exp)
 
-        xin = [keep.tile([P, TT, H // 2], BF16, name="xin%d" % hf) for hf in range(2)]
+        xin = [keep.tile([P, TT, H // 2], BF16, tag="swap%d" % hf, name="xin%d" % hf, align_bytes=64) for hf in range(2)]
         for hf in range(2):
             nc.sync.dma_start(out=xin[hf][:], in_=x_view[:, :, 1024 * hf : 1024 * hf + 1024])
 
@@ -97,17 +95,16 @@ def tile_slru_w_kernel(tc, inputs, Wi_words, Wi_scales, bi, Wo_words, Wo_scales,
         w1 = {}
         load_scales1(0)
         for j in PIECE_UNITS:
-            if j == 4:
+            if j == 3:
                 load_scales1(1)
             for g in range(G1):
                 piece = keep.tile([P, 512], U32, name="w1_%d_%d" % (j, g), align_bytes=64)
                 nc.sync.dma_start(out=piece[:].bitcast(I32), in_=w1_view[:, g, 512 * j : 512 * j + 512])
                 w1[(j, g)] = piece[:]
-        for j in CHUNK_UNITS:
-            chunk = keep.tile([P, G1, 512], U32, name="w1_c%d" % j, align_bytes=64)
-            nc.sync.dma_start(out=chunk[:].bitcast(I32), in_=w1_view[:, :, 512 * j : 512 * j + 512])
-            for g in range(G1):
-                w1[(j, g)] = chunk[:, g, :]
+        raw = {}
+        for j in W_UNITS:
+            raw[j] = keep.tile([P, G1, 512], U32, tag="swap%d" % j, name="w1_raw%d" % j, align_bytes=64)
+            nc.sync.dma_start(out=raw[j][:].bitcast(I32), in_=w1_view[:, :, 512 * j : 512 * j + 512])
         for a in range(2):
             for q in range(4):
                 nc.sync.dma_start(
@@ -115,17 +112,29 @@ def tile_slru_w_kernel(tc, inputs, Wi_words, Wi_scales, bi, Wo_words, Wo_scales,
                     in_=s2_view[4 * a : 4 * a + 4, 4 * q : 4 * q + 4, :],
                 )
         w2 = {}
-        for g in range(max(K_ROUND)):
+
+        def load_w2(g):
             tiles = [n for n in range(NT) if K_ROUND[n] > g]
-            words = keep.tile([P, 512 * len(tiles)], U32, name="w2_%d" % g, align_bytes=64)
+            if g + 2 in W_UNITS:
+                words = keep.tile([P, 512 * len(tiles)], U32, tag="swap%d" % (g + 2), name="w2_%d" % g, align_bytes=64)
+            else:
+                words = keep.tile([P, 512 * len(tiles)], U32, name="w2_%d" % g, align_bytes=64)
             nc.sync.dma_start(out=words[:].bitcast(I32), in_=w2_view[:, g, 0 : 512 * len(tiles)])
             for n in tiles:
                 w2[(g, n)] = words[:, 512 * n : 512 * n + 512]
-        for n in range(NT):
-            words = keep.tile([P, G2 - K_ROUND[n], 512], U32, name="w2_end%d" % n, align_bytes=64)
-            nc.sync.dma_start(out=words[:].bitcast(I32), in_=w2_view[:, K_ROUND[n] : G2, 512 * n : 512 * n + 512])
-            for g in range(K_ROUND[n], G2):
-                w2[(g, n)] = words[:, g - K_ROUND[n], :]
+
+        def load_w2_ends():
+            for n in range(NT):
+                if n < 2:
+                    words = keep.tile([P, G2 - K_ROUND[n], 512], U32, tag="swap%d" % n, name="w2_end%d" % n, align_bytes=64)
+                else:
+                    words = keep.tile([P, G2 - K_ROUND[n], 512], U32, name="w2_end%d" % n, align_bytes=64)
+                nc.sync.dma_start(out=words[:].bitcast(I32), in_=w2_view[:, K_ROUND[n] : G2, 512 * n : 512 * n + 512])
+                for g in range(K_ROUND[n], G2):
+                    w2[(g, n)] = words[:, g - K_ROUND[n], :]
+
+        load_w2(0)
+        load_w2(1)
 
         xt = [bank(2 + g, [P, 2, L], F32, "xt%d" % g) for g in range(G1)]
         gi = [five.tile([P, 4 * L], BF16, tag="b2k", name="gi%d" % g, align_bytes=64) for g in range(G1)]
@@ -240,7 +249,7 @@ def tile_slru_w_kernel(tc, inputs, Wi_words, Wi_scales, bi, Wo_words, Wo_scales,
                     )
 
         def scale_bias(j, t):
-            v_sb[(j, t)] = three.tile([P, L], F32, tag="v%d" % t, name="v_%d_%d" % (j, t))
+            v_sb[(j, t)] = five.tile([P, L], F32, tag="v%d" % t, name="v_%d_%d" % (j, t))
             nc.scalar.activation(
                 out=v_sb[(j, t)][:],
                 in_=vt[(j, t // 2)][:, t % 2, :],
@@ -262,47 +271,92 @@ def tile_slru_w_kernel(tc, inputs, Wi_words, Wi_scales, bi, Wo_words, Wo_scales,
             )
 
         def regroup(j):
-            xg[j] = two.tile([P, L, 4], BF16, tag="xg", name="xg%d" % j, align_bytes=64)
+            xg[j] = four.tile([P, L, 4], BF16, tag="xg", name="xg%d" % j, align_bytes=64)
             dst = xg[j][:].rearrange("p (c i) t -> p c t i", i=4)
             src = xb[j][:].rearrange("p t (c i) -> p c t i", i=4)
-            if j in VECTOR_REGROUP:
-                nc.vector.tensor_copy(out=dst, in_=src)
-            else:
-                nc.scalar.copy(out=dst, in_=src)
+            nc.scalar.copy(out=dst, in_=src)
 
         def quantise(j):
             nc.vector.quantize_mx(
                 out=xq2[j][:].bitcast(FP8X4), scales=xs2[j][:], in_=xg[j][:].rearrange("p w t -> p (w t)")
             )
 
+        pl1s = keep.tile([P, U // 2], U8, name="pl1s", align_bytes=64)
+        w1s = {}
+
+        def sort_scales():
+            nc.vector.tensor_copy(
+                out=pl1s[:].rearrange("p (j t m) -> p j m t", j=4, t=4),
+                in_=pl1[1][:].rearrange("p (j m t) -> p j m t", j=4, t=4),
+            )
+
+        def sort_words(j):
+            w1s[j] = keep.tile([P, G1, 512], U32, name="w1s%d" % j, align_bytes=64)
+            nc.vector.tensor_copy(
+                out=w1s[j][:].bitcast(I32).rearrange("p g (t m) -> p g m t", t=4),
+                in_=raw[j][:].bitcast(I32).rearrange("p g (m t) -> p g m t", t=4),
+            )
+
+        def pass1w(j, t):
+            if t % 2 == 0:
+                vt[(j, t // 2)] = bank(2 * (j - 4) + t // 2, [P, 2, L], F32, "vt_%d_%d" % (j, t // 2))
+            for g in range(G1):
+                nc.tensor.matmul_mx(
+                    out=vt[(j, t // 2)][:, t % 2, :],
+                    lhsT=w1s[j][:, g, P * t : P * t + P].bitcast(FP8X4),
+                    lhsT_scale=pl1s[4 * g : P, 512 * (j % 4) + P * t : 512 * (j % 4) + P * t + P],
+                    rhs=xq1[g][:].bitcast(FP8X4),
+                    rhs_scale=xs1[g][:],
+                    start=(g == 0),
+                    stop=(g == G1 - 1),
+                )
+
         for j in range(G2):
+            if j == 2:
+                sort_scales()
+            if j == 3:
+                sort_words(4)
+                load_w2(2)
+            if j == 4:
+                sort_words(5)
+                sort_words(6)
+                load_w2(3)
+                load_w2(4)
             if j in PIECE_UNITS:
                 order = [(tt, g) for g in range(G1) for tt in range(TT)]
-                cut = 6
-            else:
-                order = [(tt, g) for tt in range(TT) for g in range(G1)]
-                cut = 4
-            for tt, g in order[:cut]:
-                pass1(j, tt, g)
-            if j not in PIECE_UNITS:
+                for tt, g in order[:6]:
+                    pass1(j, tt, g)
+                if j >= 1:
+                    transposes(j - 1)
+                    for t in range(4):
+                        scale_bias(j - 1, t)
+                    for t in range(4):
+                        scan(j - 1, t)
+                for tt, g in order[6:]:
+                    pass1(j, tt, g)
                 sort_out(j, 0)
-            if j >= 1:
-                transposes(j - 1)
-                for t in range(4):
-                    scale_bias(j - 1, t)
+                sort_out(j, 1)
+            else:
+                pass1w(j, 0)
+                pass1w(j, 1)
+                scale_bias(j, 0)
+                scale_bias(j, 1)
+                if j - 1 in PIECE_UNITS:
+                    transposes(j - 1)
+                    for t in range(4):
+                        scale_bias(j - 1, t)
+                pass1w(j, 2)
+                pass1w(j, 3)
+                scale_bias(j, 2)
+                scale_bias(j, 3)
                 for t in range(4):
                     scan(j - 1, t)
-            for tt, g in order[cut:]:
-                pass1(j, tt, g)
-            if j in PIECE_UNITS:
-                sort_out(j, 0)
-            sort_out(j, 1)
-            if j - 3 in VECTOR_REGROUP:
-                quantise(j - 3)
-            if j - 2 in VECTOR_REGROUP:
-                regroup(j - 2)
-            if j == G2 - 1:
-                regroup(3)
+                if j == 4:
+                    sort_words(7)
+                    load_w2(5)
+                    load_w2_ends()
+                regroup(j - 4)
+                quantise(j - 4)
 
         o_ps = {}
 
@@ -325,35 +379,25 @@ def tile_slru_w_kernel(tc, inputs, Wi_words, Wi_scales, bi, Wo_words, Wo_scales,
                     pass2(tt, n, g)
 
         def finish(tt, n):
-            o_sb = eight.tile([P, 512], F32, tag="o", name="o_sb_%d_%d" % (tt, n))
+            o_sb = four.tile([P, 512], F32, tag="o", name="o_sb_%d_%d" % (tt, n))
             nc.vector.tensor_tensor(
                 out=o_sb[:], in0=o_ps[(tt, n)][:], in1=bo_bc[n // 2][:, 512 * (n % 2) : 512 * (n % 2) + 512], op=ALU.add
             )
             nc.sync.dma_start(out=out_view[:, tt, 512 * n : 512 * n + 512], in_=o_sb[:])
 
         last = G2 - 1
-        round2((0, 1), 0)
-        transposes(last)
-        for t in range(4):
-            scale_bias(last, t)
-        scan(last, 0)
-        quantise(3)
         regroup(4)
-        scan(last, 1)
-        scan(last, 2)
         quantise(4)
-        regroup(5)
-        scan(last, 3)
-        quantise(5)
-        regroup(6)
-        quantise(6)
-        regroup(7)
-        quantise(7)
-        round2((2,), 0)
-        round2((0, 1, 2), 1)
-        round2((0, 1, 2), 2)
-        for g in range(3):
+        for t in range(4):
+            scan(last, t)
+        for j in (5, 6, 7):
+            regroup(j)
+            quantise(j)
+        for g in range(2):
+            round2((0, 1, 2), g)
+        for g in range(2):
             round2((3,), g)
+        round2((0, 1, 2, 3), 2)
         for g in range(3, max(K_ROUND)):
             round2([n for n in range(NT) if K_ROUND[n] > g], g)
         for n in range(NT):

@@ -48,7 +48,7 @@ def tile_slru_w_kernel(tc, inputs, Wi_words, Wi_scales, bi, Wo_words, Wo_scales,
         w1_view = Wi_words.rearrange("g p n t -> p g (n t)").bitcast(I32)
         w2_view = Wo_words.rearrange("g p n t -> p g (n t)").bitcast(I32)
         s1_view = Wi_scales.bitcast(I32)
-        s2_view = Wo_scales.bitcast(I32)
+        s2_view = Wo_scales.bitcast(F32)
         par_view = params_log.rearrange("a (g c) -> (a g) c", c=KP)
         bi_view = bi.rearrange("(g c) -> g c", c=KP)
         bo_view = bo.rearrange("(o n) -> o n", o=1)
@@ -74,7 +74,6 @@ def tile_slru_w_kernel(tc, inputs, Wi_words, Wi_scales, bi, Wo_words, Wo_scales,
         nc.vector.memset(junk[:], 0.0)
         nc.vector.memset(pl1[0][:].bitcast(I32), 0)
         nc.vector.memset(pl1[1][:].bitcast(I32), 0)
-        nc.vector.memset(pl2[:].rearrange("p a n -> p (a n)").bitcast(I32), 0)
 
         nc.scalar.dma_start(out=bo_rows[0:1, :], in_=bo_view)
         nc.scalar.dma_start(out=par_rows[0:16, :], in_=par_view)
@@ -105,12 +104,6 @@ def tile_slru_w_kernel(tc, inputs, Wi_words, Wi_scales, bi, Wo_words, Wo_scales,
         for j in W_UNITS:
             raw[j] = keep.tile([P, G1, 512], U32, tag="swap%d" % j, name="w1_raw%d" % j, align_bytes=64)
             nc.sync.dma_start(out=raw[j][:].bitcast(I32), in_=w1_view[:, :, 512 * j : 512 * j + 512])
-        for a in range(2):
-            for q in range(4):
-                nc.sync.dma_start(
-                    out=pl2[32 * q : 32 * q + 16, a, :].bitcast(I32),
-                    in_=s2_view[4 * a : 4 * a + 4, 4 * q : 4 * q + 4, :],
-                )
         w2 = {}
 
         def load_w2(g):
@@ -210,6 +203,13 @@ def tile_slru_w_kernel(tc, inputs, Wi_words, Wi_scales, bi, Wo_words, Wo_scales,
         nc.vector.tensor_tensor(out=lam[:], in0=num[:], in1=rden[:], op=ALU.mult)
         for i in range(2):
             nc.vector.tensor_copy(out=bo_bc[i][:], in_=pb[i][:])
+        nc.vector.memset(pl2[:].rearrange("p a n -> p (a n)").bitcast(I32), 0)
+        for a in range(2):
+            for q in range(4):
+                nc.gpsimd.dma_start(
+                    out=pl2[32 * q : 32 * q + 16, a, :].bitcast(F32),
+                    in_=s2_view[4 * a : 4 * a + 4, 4 * q : 4 * q + 4, :],
+                )
 
         acc = {}
         u_sb = {}
@@ -318,9 +318,7 @@ def tile_slru_w_kernel(tc, inputs, Wi_words, Wi_scales, bi, Wo_words, Wo_scales,
                 sort_words(4)
                 load_w2(2)
             if j == 4:
-                sort_words(5)
                 sort_words(6)
-                load_w2(3)
                 load_w2(4)
             if j in PIECE_UNITS:
                 order = [(tt, g) for g in range(G1) for tt in range(TT)]
@@ -331,6 +329,9 @@ def tile_slru_w_kernel(tc, inputs, Wi_words, Wi_scales, bi, Wo_words, Wo_scales,
                     for t in range(4):
                         scale_bias(j - 1, t)
                     for t in range(4):
+                        if j == 3 and t == 2:
+                            sort_words(5)
+                            load_w2(3)
                         scan(j - 1, t)
                 for tt, g in order[6:]:
                     pass1(j, tt, g)
@@ -350,11 +351,11 @@ def tile_slru_w_kernel(tc, inputs, Wi_words, Wi_scales, bi, Wo_words, Wo_scales,
                 scale_bias(j, 2)
                 scale_bias(j, 3)
                 for t in range(4):
+                    if j == 4 and t == 2:
+                        sort_words(7)
+                        load_w2(5)
+                        load_w2_ends()
                     scan(j - 1, t)
-                if j == 4:
-                    sort_words(7)
-                    load_w2(5)
-                    load_w2_ends()
                 regroup(j - 4)
                 quantise(j - 4)
 

from contextlib import ExitStack

import concourse.mybir as mybir
from concourse.masks import make_identity

F32 = mybir.dt.float32
BF16 = mybir.dt.bfloat16
I32 = mybir.dt.int32
U32 = mybir.dt.uint32
U8 = mybir.dt.uint8
FP8X4 = mybir.dt.float8_e4m3fn_x4
ACT = mybir.ActivationFunctionType
ALU = mybir.AluOpType

P = 128
L = 256
H = 2048
U = 4096
KP = 512
TT = L // P
G1 = H // KP
G2 = U // KP
NT = H // 512

FLOPS = 2 * L * H * U * 2

PIECE_UNITS = (0, 1, 2, 3)
W_UNITS = (4, 5, 6, 7)
K_ROUND = (6, 6, 5, 5)
O_BANK = (0, 2, 4, 6)
WARM_UP = 8


def tile_slru_w_kernel(tc, inputs, Wi_words, Wi_scales, bi, Wo_words, Wo_scales, bo, params_log, out):
    nc = tc.nc
    with ExitStack() as ctx:
        keep = ctx.enter_context(tc.tile_pool(name="keep", bufs=1))
        two = ctx.enter_context(tc.tile_pool(name="two", bufs=2))
        four = ctx.enter_context(tc.tile_pool(name="four", bufs=4))
        five = ctx.enter_context(tc.tile_pool(name="five", bufs=5))
        psum = ctx.enter_context(tc.psum_pool(name="psum", bufs=1))
        ctx.enter_context(tc.manual_schedule())

        def bank(b, shape, dtype, name):
            return psum.tile(shape, dtype, tag="bank%d" % b, name=name)

        x_view = inputs.rearrange("b (tt p) k -> p (b tt) k", p=P)
        w1_view = Wi_words.rearrange("g p n t -> p g (n t)").bitcast(I32)
        w2_view = Wo_words.rearrange("g p n t -> p g (n t)").bitcast(I32)
        s1_view = Wi_scales.bitcast(I32)
        s2_view = Wo_scales.bitcast(F32)
        par_view = params_log.rearrange("a (g c) -> (a g) c", c=KP)
        bi_view = bi.rearrange("(g c) -> g c", c=KP)
        bo_view = bo.rearrange("(o n) -> o n", o=1)
        out_view = out.rearrange("b (tt p) n -> p (b tt) n", p=P)

        ident_f = keep.tile([P, P], F32, name="ident_f")
        ident_b = keep.tile([P, P], BF16, name="ident_b")
        ones_b = keep.tile([P, P], BF16, name="ones_b")
        make_identity(nc, ident_f[:])
        make_identity(nc, ident_b[:])
        nc.gpsimd.memset(ones_b[:], 1.0)

        par_rows = keep.tile([P, KP], BF16, name="par_rows")
        bo_rows = keep.tile([P, H], BF16, name="bo_rows")
        junk = keep.tile([P, 1], F32, name="junk")
        junk2 = keep.tile([P, 1], F32, name="junk2")
        pl1 = [keep.tile([P, U // 2], U8, name="pl1_%d" % hf, align_bytes=64) for hf in range(2)]
        pl2 = keep.tile([P, 2, H], U8, name="pl2", align_bytes=64)
        warm = keep.tile([P, 512], BF16, name="warm")
        nc.vector.memset(warm[:], 0.0)
        nc.vector.memset(bo_rows[:], 0.0)
        nc.vector.memset(par_rows[:], 0.0)
        nc.vector.memset(junk[:], 0.0)
        nc.vector.memset(pl1[0][:].bitcast(I32), 0)
        nc.vector.memset(pl1[1][:].bitcast(I32), 0)

        nc.scalar.dma_start(out=bo_rows[0:1, :], in_=bo_view)
        nc.scalar.dma_start(out=par_rows[0:16, :], in_=par_view)
        nc.scalar.dma_start(out=par_rows[16:24, :], in_=bi_view)
        nc.scalar.activation(out=junk2[:], in_=junk[:], func=ACT.Exp)

        xin = [keep.tile([P, TT, H // 2], BF16, tag="swap%d" % hf, name="xin%d" % hf, align_bytes=64) for hf in range(2)]
        for hf in range(2):
            nc.sync.dma_start(out=xin[hf][:], in_=x_view[:, :, 1024 * hf : 1024 * hf + 1024])

        def load_scales1(hf):
            for q in range(4):
                nc.sync.dma_start(
                    out=pl1[hf][32 * q : 32 * q + 16, :].bitcast(I32),
                    in_=s1_view[:, 4 * q : 4 * q + 4, 512 * hf : 512 * hf + 512],
                )

        w1 = {}
        load_scales1(0)
        for j in PIECE_UNITS:
            if j == 3:
                load_scales1(1)
            for g in range(G1):
                piece = keep.tile([P, 512], U32, name="w1_%d_%d" % (j, g), align_bytes=64)
                nc.sync.dma_start(out=piece[:].bitcast(I32), in_=w1_view[:, g, 512 * j : 512 * j + 512])
                w1[(j, g)] = piece[:]
        raw = {}
        for j in W_UNITS:
            raw[j] = keep.tile([P, G1, 512], U32, tag="swap%d" % j, name="w1_raw%d" % j, align_bytes=64)
            nc.sync.dma_start(out=raw[j][:].bitcast(I32), in_=w1_view[:, :, 512 * j : 512 * j + 512])
        w2 = {}

        def load_w2(g):
            tiles = [n for n in range(NT) if K_ROUND[n] > g]
            if g + 2 in W_UNITS:
                words = keep.tile([P, 512 * len(tiles)], U32, tag="swap%d" % (g + 2), name="w2_%d" % g, align_bytes=64)
            else:
                words = keep.tile([P, 512 * len(tiles)], U32, name="w2_%d" % g, align_bytes=64)
            nc.sync.dma_start(out=words[:].bitcast(I32), in_=w2_view[:, g, 0 : 512 * len(tiles)])
            for n in tiles:
                w2[(g, n)] = words[:, 512 * n : 512 * n + 512]

        def load_w2_ends():
            for n in range(NT):
                if n < 2:
                    words = keep.tile([P, G2 - K_ROUND[n], 512], U32, tag="swap%d" % n, name="w2_end%d" % n, align_bytes=64)
                else:
                    words = keep.tile([P, G2 - K_ROUND[n], 512], U32, name="w2_end%d" % n, align_bytes=64)
                nc.sync.dma_start(out=words[:].bitcast(I32), in_=w2_view[:, K_ROUND[n] : G2, 512 * n : 512 * n + 512])
                for g in range(K_ROUND[n], G2):
                    w2[(g, n)] = words[:, g - K_ROUND[n], :]

        load_w2(0)
        load_w2(1)

        xt = [bank(2 + g, [P, 2, L], F32, "xt%d" % g) for g in range(G1)]
        gi = [five.tile([P, 4 * L], BF16, tag="b2k", name="gi%d" % g, align_bytes=64) for g in range(G1)]
        xq1 = [keep.tile([P, L], U32, name="xq1_%d" % g, align_bytes=64) for g in range(G1)]
        xs1 = [keep.tile([P, L], U8, name="xs1_%d" % g, align_bytes=64) for g in range(G1)]

        def in_transposes(g):
            words = xin[g // 2][:].rearrange("p tt k -> p (tt k)").bitcast(F32)
            for u in range(2):
                for tt in range(TT):
                    base = 512 * tt + 256 * (g % 2)
                    nc.tensor.transpose(
                        out=xt[g][:, u, P * tt : P * tt + P],
                        in_=words[:, base + u : base + 256 : 2],
                        identity=ident_f[:],
                    )

        def in_regroup(g, on_vector):
            dst = gi[g][:].bitcast(F32).rearrange("p (w u) -> p w u", u=2)
            src = xt[g][:].rearrange("p u w -> p w u")
            if on_vector:
                nc.vector.tensor_copy(out=dst, in_=src)
            else:
                nc.scalar.copy(out=dst, in_=src)

        def in_quantise(g):
            nc.vector.quantize_mx(out=xq1[g][:].bitcast(FP8X4), scales=xs1[g][:], in_=gi[g][:])


        eg = keep.tile([P, 4, 16], F32, name="eg")
        th = keep.tile([P, 4, 8], F32, name="th")
        den = keep.tile([P, 4, 8], F32, name="den")
        num = keep.tile([P, 4, 8], F32, name="num")
        rden = keep.tile([P, 4, 8], F32, name="rden")
        lam = keep.tile([P, 4, 8], F32, name="lam")
        gb = keep.tile([P, 4, 8], F32, name="gb")

        warm_ps = bank(0, [P, 512], F32, "warm_ps")
        for i in range(WARM_UP):
            nc.tensor.matmul(out=warm_ps[:], lhsT=warm[:, 0:P], rhs=warm[:], start=True, stop=True)
        in_transposes(0)
        in_transposes(1)
        bo_bc = [keep.tile([P, 1024], F32, name="bo_bc%d" % i) for i in range(2)]
        pb = [bank(6 + i, [P, 1024], BF16, "pb%d" % i) for i in range(2)]
        for i in range(2):
            for k in range(2):
                nc.tensor.matmul(
                    out=pb[i][:, 512 * k : 512 * k + 512],
                    lhsT=ones_b[:],
                    rhs=bo_rows[:, 1024 * i + 512 * k : 1024 * i + 512 * k + 512],
                    start=True,
                    stop=True,
                )
        in_regroup(0, True)
        in_regroup(1, False)
        in_transposes(2)
        in_transposes(3)
        in_quantise(0)
        in_regroup(2, True)
        in_regroup(3, False)
        in_quantise(1)
        in_quantise(2)
        in_quantise(3)
        pp = bank(2, [P, 4, P], BF16, "pp")
        for t in range(4):
            nc.tensor.transpose(out=pp[:, t, :], in_=par_rows[:, t:KP:4], identity=ident_b[:])
        nc.scalar.activation(out=eg[:], in_=pp[:, :, 0:16], func=ACT.Exp)
        nc.scalar.activation(out=th[:], in_=eg[:, :, 0:8], func=ACT.Tanh, scale=0.5)
        nc.vector.tensor_tensor(out=gb[:], in0=eg[:, :, 8:16], in1=pp[:, :, 16:24], op=ALU.mult)
        nc.vector.tensor_scalar_add(out=den[:], in0=th[:], scalar1=1.0)
        nc.vector.tensor_scalar(out=num[:], in0=th[:], scalar1=-1.0, scalar2=1.0, op0=ALU.mult, op1=ALU.add)
        nc.vector.reciprocal(out=rden[:], in_=den[:])
        nc.vector.tensor_tensor(out=lam[:], in0=num[:], in1=rden[:], op=ALU.mult)
        for i in range(2):
            nc.vector.tensor_copy(out=bo_bc[i][:], in_=pb[i][:])
        nc.vector.memset(pl2[:].rearrange("p a n -> p (a n)").bitcast(I32), 0)
        for a in range(2):
            for q in range(4):
                nc.gpsimd.dma_start(
                    out=pl2[32 * q : 32 * q + 16, a, :].bitcast(F32),
                    in_=s2_view[4 * a : 4 * a + 4, 4 * q : 4 * q + 4, :],
                )

        acc = {}
        u_sb = {}
        vt = {}
        v_sb = {}
        xb = {}
        xg = {}
        xq2 = [keep.tile([P, L], U32, name="xq2_%d" % j, align_bytes=64) for j in range(G2)]
        xs2 = [keep.tile([P, L], U8, name="xs2_%d" % j, align_bytes=64) for j in range(G2)]

        def pass1(j, tt, g):
            if g == 0:
                acc[(j, tt)] = bank(2 * (j % 2) + tt, [P, 512], F32, "acc_%d_%d" % (j, tt))
            nc.tensor.matmul_mx(
                out=acc[(j, tt)][:],
                lhsT=xq1[g][:, P * tt : P * tt + P].bitcast(FP8X4),
                lhsT_scale=xs1[g][:, P * tt : P * tt + P],
                rhs=w1[(j, g)].bitcast(FP8X4),
                rhs_scale=pl1[j // 4][4 * g : P, 512 * (j % 4) : 512 * (j % 4) + 512],
                start=(g == 0),
                stop=(g == G1 - 1),
            )

        def sort_out(j, tt):
            u_sb[(j, tt)] = two.tile([P, 4, P], F32, tag="u%d" % tt, name="u_%d_%d" % (j, tt))
            nc.scalar.copy(out=u_sb[(j, tt)][:], in_=acc[(j, tt)][:].rearrange("p (c t) -> p t c", t=4))

        def transposes(j):
            for hb in range(2):
                vt[(j, hb)] = bank(4 + 2 * (j % 2) + hb, [P, 2, L], F32, "vt_%d_%d" % (j, hb))
            for t in range(4):
                for tt in range(TT):
                    nc.tensor.transpose(
                        out=vt[(j, t // 2)][:, t % 2, P * tt : P * tt + P],
                        in_=u_sb[(j, tt)][:, t, :],
                        identity=ident_f[:],
                    )

        def scale_bias(j, t):
            v_sb[(j, t)] = five.tile([P, L], F32, tag="v%d" % t, name="v_%d_%d" % (j, t))
            nc.scalar.activation(
                out=v_sb[(j, t)][:],
                in_=vt[(j, t // 2)][:, t % 2, :],
                func=ACT.Identity,
                bias=gb[:, t, j : j + 1],
                scale=eg[:, t, 8 + j : 9 + j],
            )

        def scan(j, t):
            if t == 0:
                xb[j] = five.tile([P, 4, L], BF16, tag="b2k", name="xb%d" % j, align_bytes=64)
            nc.vector.tensor_tensor_scan(
                out=xb[j][:, t, :],
                data0=lam[:, t, j : j + 1].to_broadcast([P, L]),
                data1=v_sb[(j, t)][:],
                initial=0.0,
                op0=ALU.mult,
                op1=ALU.add,
            )

        def regroup(j):
            xg[j] = four.tile([P, L, 4], BF16, tag="xg", name="xg%d" % j, align_bytes=64)
            dst = xg[j][:].rearrange("p (c i) t -> p c t i", i=4)
            src = xb[j][:].rearrange("p t (c i) -> p c t i", i=4)
            nc.scalar.copy(out=dst, in_=src)

        def quantise(j):
            nc.vector.quantize_mx(
                out=xq2[j][:].bitcast(FP8X4), scales=xs2[j][:], in_=xg[j][:].rearrange("p w t -> p (w t)")
            )

        pl1s = keep.tile([P, U // 2], U8, name="pl1s", align_bytes=64)
        w1s = {}

        def sort_scales():
            nc.vector.tensor_copy(
                out=pl1s[:].rearrange("p (j t m) -> p j m t", j=4, t=4),
                in_=pl1[1][:].rearrange("p (j m t) -> p j m t", j=4, t=4),
            )

        def sort_words(j):
            w1s[j] = keep.tile([P, G1, 512], U32, name="w1s%d" % j, align_bytes=64)
            nc.vector.tensor_copy(
                out=w1s[j][:].bitcast(I32).rearrange("p g (t m) -> p g m t", t=4),
                in_=raw[j][:].bitcast(I32).rearrange("p g (m t) -> p g m t", t=4),
            )

        def pass1w(j, t):
            if t % 2 == 0:
                vt[(j, t // 2)] = bank(2 * (j - 4) + t // 2, [P, 2, L], F32, "vt_%d_%d" % (j, t // 2))
            for g in range(G1):
                nc.tensor.matmul_mx(
                    out=vt[(j, t // 2)][:, t % 2, :],
                    lhsT=w1s[j][:, g, P * t : P * t + P].bitcast(FP8X4),
                    lhsT_scale=pl1s[4 * g : P, 512 * (j % 4) + P * t : 512 * (j % 4) + P * t + P],
                    rhs=xq1[g][:].bitcast(FP8X4),
                    rhs_scale=xs1[g][:],
                    start=(g == 0),
                    stop=(g == G1 - 1),
                )

        for j in range(G2):
            if j == 2:
                sort_scales()
            if j == 3:
                sort_words(4)
                load_w2(2)
            if j == 4:
                sort_words(6)
                load_w2(4)
            if j in PIECE_UNITS:
                order = [(tt, g) for g in range(G1) for tt in range(TT)]
                for tt, g in order[:6]:
                    pass1(j, tt, g)
                if j >= 1:
                    transposes(j - 1)
                    for t in range(4):
                        scale_bias(j - 1, t)
                    for t in range(4):
                        if j == 3 and t == 2:
                            sort_words(5)
                            load_w2(3)
                        scan(j - 1, t)
                for tt, g in order[6:]:
                    pass1(j, tt, g)
                sort_out(j, 0)
                sort_out(j, 1)
            else:
                pass1w(j, 0)
                pass1w(j, 1)
                scale_bias(j, 0)
                scale_bias(j, 1)
                if j - 1 in PIECE_UNITS:
                    transposes(j - 1)
                    for t in range(4):
                        scale_bias(j - 1, t)
                pass1w(j, 2)
                pass1w(j, 3)
                scale_bias(j, 2)
                scale_bias(j, 3)
                for t in range(4):
                    if j == 4 and t == 2:
                        sort_words(7)
                        load_w2(5)
                        load_w2_ends()
                    scan(j - 1, t)
                regroup(j - 4)
                quantise(j - 4)

        o_ps = {}

        def pass2(tt, n, g):
            if g == 0:
                o_ps[(tt, n)] = bank(O_BANK[n] + tt, [P, 512], F32, "o_%d_%d" % (tt, n))
            nc.tensor.matmul_mx(
                out=o_ps[(tt, n)][:],
                lhsT=xq2[g][:, P * tt : P * tt + P].bitcast(FP8X4),
                lhsT_scale=xs2[g][:, P * tt : P * tt + P],
                rhs=w2[(g, n)].bitcast(FP8X4),
                rhs_scale=pl2[4 * (g % 4) : P, g // 4, 512 * n : 512 * n + 512],
                start=(g == 0),
                stop=(g == G2 - 1),
            )

        def round2(tiles, g):
            for n in tiles:
                for tt in range(TT):
                    pass2(tt, n, g)

        def finish(tt, n):
            o_sb = four.tile([P, 512], F32, tag="o", name="o_sb_%d_%d" % (tt, n))
            nc.vector.tensor_tensor(
                out=o_sb[:], in0=o_ps[(tt, n)][:], in1=bo_bc[n // 2][:, 512 * (n % 2) : 512 * (n % 2) + 512], op=ALU.add
            )
            nc.sync.dma_start(out=out_view[:, tt, 512 * n : 512 * n + 512], in_=o_sb[:])

        last = G2 - 1
        regroup(4)
        quantise(4)
        for t in range(4):
            scan(last, t)
        for j in (5, 6, 7):
            regroup(j)
            quantise(j)
        for g in range(2):
            round2((0, 1, 2), g)
        for g in range(2):
            round2((3,), g)
        round2((0, 1, 2, 3), 2)
        for g in range(3, max(K_ROUND)):
            round2([n for n in range(NT) if K_ROUND[n] > g], g)
        for n in range(NT):
            for tt in range(TT):
                for g in range(K_ROUND[n], G2):
                    pass2(tt, n, g)
                finish(tt, n)
